import numpy as np
import ml_dtypes

BF16 = ml_dtypes.bfloat16


def bf(x):
    return np.asarray(x, np.float32).astype(BF16)


def f32(x):
    return np.asarray(x, np.float32)


def f64(x):
    return np.asarray(x).astype(np.float64)


def striped(idx):
    return np.tile(idx.reshape(-1, 16).T, (8, 1))


C, S, H, W, GH, N = 128, 1024, 32, 64, 128, 2048
OFFSETS = [(-4, -4), (-4, -1), (-4, 2), (-3, 4), (-2, -3), (2, 3), (3, -2), (4, 4)]


def sigmoid(v):
    return 1.0 / (1.0 + np.exp(-v))


def setup_inputs():
    return {
        "table": bf(np.random.standard_normal((C, S))),
        "wm": bf(2.0 * np.random.standard_normal((C, C)) / np.sqrt(C)),
        "bm": f32(0.1 * np.random.standard_normal((C, 1))),
        "wx": bf(np.random.standard_normal((C, GH)) / np.sqrt(C + C)),
        "wa": bf(np.random.standard_normal((C, GH)) / np.sqrt(C + C)),
        "bh": f32(0.1 * np.random.standard_normal((GH, 1))),
        "wz": bf(2.0 * np.random.standard_normal((GH, C)) / np.sqrt(GH)),
        "bz": f32(0.1 * np.random.standard_normal((C, 1))),
        "offs": striped(np.random.permutation(np.tile(np.arange(S), 2))[:N]),
    }


def reference(table, wm, bm, wx, wa, bh, wz, bz, offs):
    idx = offs[:16].T.reshape(-1)
    xp = f64(table)[:, idx]
    msg = (f64(wm).T @ xp + f64(bm)).reshape(C, H, W)
    agg = np.zeros((C, H, W), np.float64)
    for dy, dx in OFFSETS:
        agg = agg + np.roll(msg, (dy, dx), axis=(1, 2))
    agg = agg.reshape(C, N) / len(OFFSETS)
    hidden = np.maximum(f64(wx).T @ xp + f64(wa).T @ agg + f64(bh), 0.0)
    gate = sigmoid(f64(wz).T @ hidden + f64(bz))
    return agg * gate

@@ -1,0 +1,119 @@
+import concourse.mybir as mybir
+
+F32 = mybir.dt.float32
+BF16 = mybir.dt.bfloat16
+U16 = mybir.dt.uint16
+ACT = mybir.ActivationFunctionType
+ALU = mybir.AluOpType
+
+P = 128
+TABLE_COLS = 1024
+GRID_ROWS, GRID_COLS = 32, 64
+N = GRID_ROWS * GRID_COLS
+PIECE = 512
+PIECE_ROWS = PIECE // GRID_COLS
+N_PIECES = N // PIECE
+PIECE_OFFSETS = PIECE // 16
+SHIFTS = ((-4, -4), (-4, -1), (-4, 2), (-3, 4), (-2, -3), (2, 3), (3, -2), (4, 4))
+REACH = 4
+LEFT = 8
+PAD_ROWS = GRID_ROWS + 2 * REACH
+PAD_COLS = LEFT + GRID_COLS + LEFT
+
+FLOPS = 4 * 2 * P * P * N
+
+
+def as_grid(flat):
+    return flat.rearrange("p (r t) -> p r t", t=GRID_COLS)
+
+
+def shifted(msg_pad, q, dy, dx):
+    row = REACH + q * PIECE_ROWS - dy
+    col = LEFT - dx
+    return msg_pad[:, row : row + PIECE_ROWS, col : col + GRID_COLS]
+
+
+def tile_graphaugmentation_kernel(tc, table, wm, bm, wx, wa, bh, wz, bz, offs, out):
+    nc = tc.nc
+    with (
+        tc.tile_pool(name="held", bufs=1) as held,
+        tc.tile_pool(name="work", bufs=N_PIECES) as work,
+        tc.psum_pool(name="psum_hidden", bufs=N_PIECES) as psum_hidden,
+        tc.psum_pool(name="psum_turn", bufs=N_PIECES) as psum_turn,
+    ):
+        offsets = held.tile([P, N // 16], U16, name="offsets")
+        nc.sync.dma_start(offsets[:], offs)
+        table_sb = held.tile([P, TABLE_COLS], BF16, name="table_sb")
+        nc.scalar.dma_start(table_sb[:], table)
+        wm_sb = held.tile([P, P], BF16, name="wm_sb")
+        nc.sync.dma_start(wm_sb[:], wm)
+        bm_sb = held.tile([P, 1], F32, name="bm_sb")
+        nc.scalar.dma_start(bm_sb[:], bm)
+        wx_sb = held.tile([P, P], BF16, name="wx_sb")
+        nc.sync.dma_start(wx_sb[:], wx)
+        wa_sb = held.tile([P, P], BF16, name="wa_sb")
+        nc.gpsimd.dma_start(wa_sb[:], wa)
+        bh_sb = held.tile([P, 1], F32, name="bh_sb")
+        nc.gpsimd.dma_start(bh_sb[:], bh)
+        wz_sb = held.tile([P, P], BF16, name="wz_sb")
+        nc.gpsimd.dma_start(wz_sb[:], wz)
+        bz_sb = held.tile([P, 1], F32, name="bz_sb")
+        nc.gpsimd.dma_start(bz_sb[:], bz)
+
+        warm = held.tile([P, 1], F32, name="warm")
+        nc.vector.memset(warm[:], 0.0)
+        nc.scalar.activation(warm[:], warm[:], ACT.Sigmoid)
+
+        share = 1.0 / len(SHIFTS)
+        bm_share = held.tile([P, 1], F32, name="bm_share")
+        nc.vector.tensor_scalar_mul(bm_share[:], bm_sb[:], share)
+
+        msg_pad = held.tile([P, PAD_ROWS, PAD_COLS], F32, name="msg_pad")
+        first, last = LEFT, LEFT + GRID_COLS
+        for q in range(N_PIECES):
+            picked = table_sb[:].indirect(offsets[:, q * PIECE_OFFSETS : (q + 1) * PIECE_OFFSETS])
+            msg_ps = psum_turn.tile([P, PIECE], F32, name="msg_ps", tag="turn")
+            nc.tensor.matmul(msg_ps[:], wm_sb[:], picked, start=True, stop=True)
+            rows = msg_pad[:, REACH + q * PIECE_ROWS : REACH + (q + 1) * PIECE_ROWS, :]
+            nc.scalar.activation(
+                rows[:, :, first:last], as_grid(msg_ps[:]), ACT.Identity, bias=bm_share[:], scale=share
+            )
+            nc.vector.tensor_copy(rows[:, :, first - REACH : first], rows[:, :, last - REACH : last])
+            nc.vector.tensor_copy(rows[:, :, last : last + REACH], rows[:, :, first : first + REACH])
+        used = slice(first - REACH, last + REACH)
+        nc.vector.tensor_copy(msg_pad[:, 0:REACH, used], msg_pad[:, GRID_ROWS : GRID_ROWS + REACH, used])
+        nc.vector.tensor_copy(
+            msg_pad[:, REACH + GRID_ROWS : PAD_ROWS, used], msg_pad[:, REACH : 2 * REACH, used]
+        )
+
+        hidden_ps = []
+        for q in range(N_PIECES):
+            picked = table_sb[:].indirect(offsets[:, q * PIECE_OFFSETS : (q + 1) * PIECE_OFFSETS])
+            hidden_ps.append(psum_hidden.tile([P, PIECE], F32, name="hidden_ps"))
+            nc.tensor.matmul(hidden_ps[q][:], wx_sb[:], picked, start=True, stop=False)
+
+        for q in range(N_PIECES):
+            pairs = []
+            for i in range(0, len(SHIFTS), 2):
+                pair = work.tile([P, PIECE], F32, name=f"pair{i // 2}")
+                nc.vector.tensor_tensor(
+                    as_grid(pair[:]), shifted(msg_pad, q, *SHIFTS[i]), shifted(msg_pad, q, *SHIFTS[i + 1]), ALU.add
+                )
+                pairs.append(pair)
+            nc.vector.tensor_tensor(pairs[0][:], pairs[0][:], pairs[1][:], ALU.add)
+            nc.vector.tensor_tensor(pairs[2][:], pairs[2][:], pairs[3][:], ALU.add)
+            agg = work.tile([P, PIECE], F32, name="agg")
+            nc.vector.tensor_tensor(agg[:], pairs[0][:], pairs[2][:], ALU.add)
+
+            agg_bf = work.tile([P, PIECE], BF16, name="agg_bf")
+            nc.scalar.copy(agg_bf[:], agg[:])
+            nc.tensor.matmul(hidden_ps[q][:], wa_sb[:], agg_bf[:], start=False, stop=True)
+            hidden_bf = work.tile([P, PIECE], BF16, name="hidden_bf")
+            nc.scalar.activation(hidden_bf[:], hidden_ps[q][:], ACT.Relu, bias=bh_sb[:])
+            gate_ps = psum_turn.tile([P, PIECE], F32, name="gate_ps", tag="turn")
+            nc.tensor.matmul(gate_ps[:], wz_sb[:], hidden_bf[:], start=True, stop=True)
+            gate = work.tile([P, PIECE], F32, name="gate")
+            nc.scalar.activation(gate[:], gate_ps[:], ACT.Sigmoid, bias=bz_sb[:])
+            gated = work.tile([P, PIECE], F32, name="gated")
+            nc.vector.tensor_tensor(gated[:], agg[:], gate[:], ALU.mult)
+            nc.sync.dma_start(out[:, q * PIECE : (q + 1) * PIECE], gated[:])

@@ -14,7 +14,10 @@ PIECE = 512
 PIECE_ROWS = PIECE // GRID_COLS
 N_PIECES = N // PIECE
 PIECE_OFFSETS = PIECE // 16
-SHIFTS = ((-4, -4), (-4, -1), (-4, 2), (-3, 4), (-2, -3), (2, 3), (3, -2), (4, 4))
+STEP = (2, 1)
+DUO_SHIFTS = ((-4, -4), (2, 3))
+LONE_SHIFTS = ((-4, -1), (-4, 2), (-3, 4), (3, -2))
+N_SHIFTS = 2 * len(DUO_SHIFTS) + len(LONE_SHIFTS)
 REACH = 4
 LEFT = 8
 PAD_ROWS = GRID_ROWS + 2 * REACH
@@ -27,10 +30,10 @@ def as_grid(flat):
     return flat.rearrange("p (r t) -> p r t", t=GRID_COLS)
 
 
-def shifted(msg_pad, q, dy, dx):
+def shifted(padded, q, dy, dx):
     row = REACH + q * PIECE_ROWS - dy
     col = LEFT - dx
-    return msg_pad[:, row : row + PIECE_ROWS, col : col + GRID_COLS]
+    return padded[:, row : row + PIECE_ROWS, col : col + GRID_COLS]
 
 
 def tile_graphaugmentation_kernel(tc, table, wm, bm, wx, wa, bh, wz, bz, offs, out):
@@ -64,13 +67,14 @@ def tile_graphaugmentation_kernel(tc, table, wm, bm, wx, wa, bh, wz, bz, offs, o
         nc.vector.memset(warm[:], 0.0)
         nc.scalar.activation(warm[:], warm[:], ACT.Sigmoid)
 
-        share = 1.0 / len(SHIFTS)
+        share = 1.0 / N_SHIFTS
         bm_share = held.tile([P, 1], F32, name="bm_share")
         nc.vector.tensor_scalar_mul(bm_share[:], bm_sb[:], share)
 
         msg_pad = held.tile([P, PAD_ROWS, PAD_COLS], F32, name="msg_pad")
         first, last = LEFT, LEFT + GRID_COLS
-        for q in range(N_PIECES):
+        used = slice(first - REACH, last + REACH)
+        for q in (N_PIECES - 1, *range(N_PIECES - 1)):
             picked = table_sb[:].indirect(offsets[:, q * PIECE_OFFSETS : (q + 1) * PIECE_OFFSETS])
             msg_ps = psum_turn.tile([P, PIECE], F32, name="msg_ps", tag="turn")
             nc.tensor.matmul(msg_ps[:], wm_sb[:], picked, start=True, stop=True)
@@ -80,11 +84,12 @@ def tile_graphaugmentation_kernel(tc, table, wm, bm, wx, wa, bh, wz, bz, offs, o
             )
             nc.vector.tensor_copy(rows[:, :, first - REACH : first], rows[:, :, last - REACH : last])
             nc.vector.tensor_copy(rows[:, :, last : last + REACH], rows[:, :, first : first + REACH])
-        used = slice(first - REACH, last + REACH)
-        nc.vector.tensor_copy(msg_pad[:, 0:REACH, used], msg_pad[:, GRID_ROWS : GRID_ROWS + REACH, used])
-        nc.vector.tensor_copy(
-            msg_pad[:, REACH + GRID_ROWS : PAD_ROWS, used], msg_pad[:, REACH : 2 * REACH, used]
-        )
+            if q == N_PIECES - 1:
+                nc.vector.tensor_copy(msg_pad[:, 0:REACH, used], msg_pad[:, GRID_ROWS : GRID_ROWS + REACH, used])
+            if q == 0:
+                nc.vector.tensor_copy(
+                    msg_pad[:, REACH + GRID_ROWS : PAD_ROWS, used], msg_pad[:, REACH : 2 * REACH, used]
+                )
 
         hidden_ps = []
         for q in range(N_PIECES):
@@ -92,18 +97,40 @@ def tile_graphaugmentation_kernel(tc, table, wm, bm, wx, wa, bh, wz, bz, offs, o
             hidden_ps.append(psum_hidden.tile([P, PIECE], F32, name="hidden_ps"))
             nc.tensor.matmul(hidden_ps[q][:], wx_sb[:], picked, start=True, stop=False)
 
+        duo_pad = held.tile([P, PAD_ROWS, PAD_COLS], F32, name="duo_pad")
+        duo_cols = slice(first - REACH + STEP[1], last + REACH)
+        back_cols = slice(first - REACH, last + REACH - STEP[1])
+
+        def make_duo_block(b):
+            top = STEP[0] + b * PIECE_ROWS
+            end = min(top + PIECE_ROWS, PAD_ROWS)
+            nc.vector.tensor_tensor(
+                duo_pad[:, top:end, duo_cols],
+                msg_pad[:, top:end, duo_cols],
+                msg_pad[:, top - STEP[0] : end - STEP[0], back_cols],
+                ALU.add,
+            )
+
+        make_duo_block(0)
+        make_duo_block(1)
         for q in range(N_PIECES):
-            pairs = []
-            for i in range(0, len(SHIFTS), 2):
-                pair = work.tile([P, PIECE], F32, name=f"pair{i // 2}")
-                nc.vector.tensor_tensor(
-                    as_grid(pair[:]), shifted(msg_pad, q, *SHIFTS[i]), shifted(msg_pad, q, *SHIFTS[i + 1]), ALU.add
-                )
-                pairs.append(pair)
-            nc.vector.tensor_tensor(pairs[0][:], pairs[0][:], pairs[1][:], ALU.add)
-            nc.vector.tensor_tensor(pairs[2][:], pairs[2][:], pairs[3][:], ALU.add)
+            lone01 = work.tile([P, PIECE], F32, name="lone01")
+            nc.vector.tensor_tensor(
+                as_grid(lone01[:]), shifted(msg_pad, q, *LONE_SHIFTS[0]), shifted(msg_pad, q, *LONE_SHIFTS[1]), ALU.add
+            )
+            lone23 = work.tile([P, PIECE], F32, name="lone23")
+            nc.vector.tensor_tensor(
+                as_grid(lone23[:]), shifted(msg_pad, q, *LONE_SHIFTS[2]), shifted(msg_pad, q, *LONE_SHIFTS[3]), ALU.add
+            )
+            duos = work.tile([P, PIECE], F32, name="duos")
+            nc.vector.tensor_tensor(
+                as_grid(duos[:]), shifted(duo_pad, q, *DUO_SHIFTS[0]), shifted(duo_pad, q, *DUO_SHIFTS[1]), ALU.add
+            )
+            nc.vector.tensor_tensor(lone01[:], lone01[:], lone23[:], ALU.add)
+            if q + 2 <= N_PIECES:
+                make_duo_block(q + 2)
             agg = work.tile([P, PIECE], F32, name="agg")
-            nc.vector.tensor_tensor(agg[:], pairs[0][:], pairs[2][:], ALU.add)
+            nc.vector.tensor_tensor(agg[:], duos[:], lone01[:], ALU.add)
 
             agg_bf = work.tile([P, PIECE], BF16, name="agg_bf")
             nc.scalar.copy(agg_bf[:], agg[:])

@@ -10,10 +10,11 @@ P = 128
 TABLE_COLS = 1024
 GRID_ROWS, GRID_COLS = 32, 64
 N = GRID_ROWS * GRID_COLS
-PIECE = 512
-PIECE_ROWS = PIECE // GRID_COLS
-N_PIECES = N // PIECE
-PIECE_OFFSETS = PIECE // 16
+ROW_OFFSETS = GRID_COLS // 16
+BANK_ROWS = 512 // GRID_COLS
+N_BANKS = GRID_ROWS // BANK_ROWS
+PIECES = ((0, 8), (8, 8), (16, 8), (24, 4), (28, 4))
+
 STEP = (2, 1)
 DUO_SHIFTS = ((-4, -4), (2, 3))
 LONE_SHIFTS = ((-4, -1), (-4, 2), (-3, 4), (3, -2))
@@ -22,6 +23,7 @@ REACH = 4
 LEFT = 8
 PAD_ROWS = GRID_ROWS + 2 * REACH
 PAD_COLS = LEFT + GRID_COLS + LEFT
+N_DUO_BLOCKS = (PAD_ROWS - STEP[0] + BANK_ROWS - 1) // BANK_ROWS
 
 FLOPS = 4 * 2 * P * P * N
 
@@ -30,19 +32,21 @@ def as_grid(flat):
     return flat.rearrange("p (r t) -> p r t", t=GRID_COLS)
 
 
-def shifted(padded, q, dy, dx):
-    row = REACH + q * PIECE_ROWS - dy
+def shifted(padded, piece, shift):
+    top, n_rows = piece
+    dy, dx = shift
+    row = REACH + top - dy
     col = LEFT - dx
-    return padded[:, row : row + PIECE_ROWS, col : col + GRID_COLS]
+    return padded[:, row : row + n_rows, col : col + GRID_COLS]
 
 
 def tile_graphaugmentation_kernel(tc, table, wm, bm, wx, wa, bh, wz, bz, offs, out):
     nc = tc.nc
     with (
         tc.tile_pool(name="held", bufs=1) as held,
-        tc.tile_pool(name="work", bufs=N_PIECES) as work,
-        tc.psum_pool(name="psum_hidden", bufs=N_PIECES) as psum_hidden,
-        tc.psum_pool(name="psum_turn", bufs=N_PIECES) as psum_turn,
+        tc.tile_pool(name="work", bufs=len(PIECES)) as work,
+        tc.psum_pool(name="psum_hidden", bufs=len(PIECES)) as psum_hidden,
+        tc.psum_pool(name="psum_turn", bufs=8 - len(PIECES)) as psum_turn,
     ):
         offsets = held.tile([P, N // 16], U16, name="offsets")
         nc.sync.dma_start(offsets[:], offs)
@@ -54,14 +58,14 @@ def tile_graphaugmentation_kernel(tc, table, wm, bm, wx, wa, bh, wz, bz, offs, o
         nc.scalar.dma_start(bm_sb[:], bm)
         wx_sb = held.tile([P, P], BF16, name="wx_sb")
         nc.sync.dma_start(wx_sb[:], wx)
-        wa_sb = held.tile([P, P], BF16, name="wa_sb")
-        nc.gpsimd.dma_start(wa_sb[:], wa)
         bh_sb = held.tile([P, 1], F32, name="bh_sb")
-        nc.gpsimd.dma_start(bh_sb[:], bh)
-        wz_sb = held.tile([P, P], BF16, name="wz_sb")
-        nc.gpsimd.dma_start(wz_sb[:], wz)
+        nc.scalar.dma_start(bh_sb[:], bh)
+        wa_sb = held.tile([P, P], BF16, name="wa_sb")
+        nc.sync.dma_start(wa_sb[:], wa)
         bz_sb = held.tile([P, 1], F32, name="bz_sb")
-        nc.gpsimd.dma_start(bz_sb[:], bz)
+        nc.scalar.dma_start(bz_sb[:], bz)
+        wz_sb = held.tile([P, P], BF16, name="wz_sb")
+        nc.sync.dma_start(wz_sb[:], wz)
 
         warm = held.tile([P, 1], F32, name="warm")
         nc.vector.memset(warm[:], 0.0)
@@ -71,39 +75,56 @@ def tile_graphaugmentation_kernel(tc, table, wm, bm, wx, wa, bh, wz, bz, offs, o
         bm_share = held.tile([P, 1], F32, name="bm_share")
         nc.vector.tensor_scalar_mul(bm_share[:], bm_sb[:], share)
 
+        def picked(top, n_rows):
+            return table_sb[:].indirect(offsets[:, top * ROW_OFFSETS : (top + n_rows) * ROW_OFFSETS])
+
         msg_pad = held.tile([P, PAD_ROWS, PAD_COLS], F32, name="msg_pad")
         first, last = LEFT, LEFT + GRID_COLS
         used = slice(first - REACH, last + REACH)
-        for q in (N_PIECES - 1, *range(N_PIECES - 1)):
-            picked = table_sb[:].indirect(offsets[:, q * PIECE_OFFSETS : (q + 1) * PIECE_OFFSETS])
-            msg_ps = psum_turn.tile([P, PIECE], F32, name="msg_ps", tag="turn")
-            nc.tensor.matmul(msg_ps[:], wm_sb[:], picked, start=True, stop=True)
-            rows = msg_pad[:, REACH + q * PIECE_ROWS : REACH + (q + 1) * PIECE_ROWS, :]
+
+        def make_msg_bank(b):
+            msg_ps = psum_turn.tile([P, BANK_ROWS * GRID_COLS], F32, name="msg_ps", tag="turn")
+            nc.tensor.matmul(msg_ps[:], wm_sb[:], picked(b * BANK_ROWS, BANK_ROWS), start=True, stop=True)
             nc.scalar.activation(
-                rows[:, :, first:last], as_grid(msg_ps[:]), ACT.Identity, bias=bm_share[:], scale=share
+                msg_pad[:, REACH + b * BANK_ROWS : REACH + (b + 1) * BANK_ROWS, first:last],
+                as_grid(msg_ps[:]),
+                ACT.Identity,
+                bias=bm_share[:],
+                scale=share,
             )
+
+        make_msg_bank(N_BANKS - 1)
+        make_msg_bank(0)
+        make_msg_bank(1)
+
+        hidden_ps = []
+        for top, n_rows in PIECES:
+            hidden_ps.append(psum_hidden.tile([P, n_rows * GRID_COLS], F32, name="hidden_ps"))
+            nc.tensor.matmul(hidden_ps[-1][:], wx_sb[:], picked(top, n_rows), start=True, stop=False)
+
+        make_msg_bank(2)
+
+
+        def pad_msg_bank(b):
+            rows = msg_pad[:, REACH + b * BANK_ROWS : REACH + (b + 1) * BANK_ROWS, :]
             nc.vector.tensor_copy(rows[:, :, first - REACH : first], rows[:, :, last - REACH : last])
             nc.vector.tensor_copy(rows[:, :, last : last + REACH], rows[:, :, first : first + REACH])
-            if q == N_PIECES - 1:
+            if b == N_BANKS - 1:
                 nc.vector.tensor_copy(msg_pad[:, 0:REACH, used], msg_pad[:, GRID_ROWS : GRID_ROWS + REACH, used])
-            if q == 0:
+            if b == 0:
                 nc.vector.tensor_copy(
                     msg_pad[:, REACH + GRID_ROWS : PAD_ROWS, used], msg_pad[:, REACH : 2 * REACH, used]
                 )
-
-        hidden_ps = []
-        for q in range(N_PIECES):
-            picked = table_sb[:].indirect(offsets[:, q * PIECE_OFFSETS : (q + 1) * PIECE_OFFSETS])
-            hidden_ps.append(psum_hidden.tile([P, PIECE], F32, name="hidden_ps"))
-            nc.tensor.matmul(hidden_ps[q][:], wx_sb[:], picked, start=True, stop=False)
 
         duo_pad = held.tile([P, PAD_ROWS, PAD_COLS], F32, name="duo_pad")
         duo_cols = slice(first - REACH + STEP[1], last + REACH)
         back_cols = slice(first - REACH, last + REACH - STEP[1])
 
         def make_duo_block(b):
-            top = STEP[0] + b * PIECE_ROWS
-            end = min(top + PIECE_ROWS, PAD_ROWS)
+            if b < N_BANKS - 1:
+                pad_msg_bank(b)
+            top = STEP[0] + b * BANK_ROWS
+            end = min(top + BANK_ROWS, PAD_ROWS)
             nc.vector.tensor_tensor(
                 duo_pad[:, top:end, duo_cols],
                 msg_pad[:, top:end, duo_cols],
@@ -111,36 +132,53 @@ def tile_graphaugmentation_kernel(tc, table, wm, bm, wx, wa, bh, wz, bz, offs, o
                 ALU.add,
             )
 
+        def first_half_of_gate(i, agg_bf):
+            nc.tensor.matmul(hidden_ps[i][:], wa_sb[:], agg_bf[:], start=False, stop=True)
+            hidden_bf = work.tile([P, PIECES[i][1] * GRID_COLS], BF16, name="hidden_bf")
+            nc.scalar.activation(hidden_bf[:], hidden_ps[i][:], ACT.Relu, bias=bh_sb[:])
+            return hidden_bf
+
+        def second_half_of_gate(i, hidden_bf):
+            cells = PIECES[i][1] * GRID_COLS
+            gate_ps = psum_turn.tile([P, cells], F32, name="gate_ps", tag="turn")
+            nc.tensor.matmul(gate_ps[:], wz_sb[:], hidden_bf[:], start=True, stop=True)
+            gate = work.tile([P, cells], F32, name="gate")
+            nc.scalar.activation(gate[:], gate_ps[:], ACT.Sigmoid, bias=bz_sb[:])
+            return gate
+
+        aggs, hiddens, gates = [], [], []
+        pad_msg_bank(N_BANKS - 1)
         make_duo_block(0)
         make_duo_block(1)
-        for q in range(N_PIECES):
-            lone01 = work.tile([P, PIECE], F32, name="lone01")
+        for i, piece in enumerate(PIECES):
+            cells = piece[1] * GRID_COLS
+            lone01 = work.tile([P, cells], F32, name="lone01")
             nc.vector.tensor_tensor(
-                as_grid(lone01[:]), shifted(msg_pad, q, *LONE_SHIFTS[0]), shifted(msg_pad, q, *LONE_SHIFTS[1]), ALU.add
+                as_grid(lone01[:]), shifted(msg_pad, piece, LONE_SHIFTS[0]), shifted(msg_pad, piece, LONE_SHIFTS[1]), ALU.add
             )
-            lone23 = work.tile([P, PIECE], F32, name="lone23")
+            lone23 = work.tile([P, cells], F32, name="lone23")
             nc.vector.tensor_tensor(
-                as_grid(lone23[:]), shifted(msg_pad, q, *LONE_SHIFTS[2]), shifted(msg_pad, q, *LONE_SHIFTS[3]), ALU.add
+                as_grid(lone23[:]), shifted(msg_pad, piece, LONE_SHIFTS[2]), shifted(msg_pad, piece, LONE_SHIFTS[3]), ALU.add
             )
-            duos = work.tile([P, PIECE], F32, name="duos")
+            duos = work.tile([P, cells], F32, name="duos")
             nc.vector.tensor_tensor(
-                as_grid(duos[:]), shifted(duo_pad, q, *DUO_SHIFTS[0]), shifted(duo_pad, q, *DUO_SHIFTS[1]), ALU.add
+                as_grid(duos[:]), shifted(duo_pad, piece, DUO_SHIFTS[0]), shifted(duo_pad, piece, DUO_SHIFTS[1]), ALU.add
             )
             nc.vector.tensor_tensor(lone01[:], lone01[:], lone23[:], ALU.add)
-            if q + 2 <= N_PIECES:
-                make_duo_block(q + 2)
-            agg = work.tile([P, PIECE], F32, name="agg")
+            if i + 2 < N_DUO_BLOCKS:
+                make_duo_block(i + 2)
+            agg = work.tile([P, cells], F32, name="agg")
             nc.vector.tensor_tensor(agg[:], duos[:], lone01[:], ALU.add)
+            aggs.append(agg)
+            agg_bf = work.tile([P, cells], BF16, name="agg_bf")
+            nc.vector.tensor_copy(agg_bf[:], agg[:])
 
-            agg_bf = work.tile([P, PIECE], BF16, name="agg_bf")
-            nc.scalar.copy(agg_bf[:], agg[:])
-            nc.tensor.matmul(hidden_ps[q][:], wa_sb[:], agg_bf[:], start=False, stop=True)
-            hidden_bf = work.tile([P, PIECE], BF16, name="hidden_bf")
-            nc.scalar.activation(hidden_bf[:], hidden_ps[q][:], ACT.Relu, bias=bh_sb[:])
-            gate_ps = psum_turn.tile([P, PIECE], F32, name="gate_ps", tag="turn")
-            nc.tensor.matmul(gate_ps[:], wz_sb[:], hidden_bf[:], start=True, stop=True)
-            gate = work.tile([P, PIECE], F32, name="gate")
-            nc.scalar.activation(gate[:], gate_ps[:], ACT.Sigmoid, bias=bz_sb[:])
-            gated = work.tile([P, PIECE], F32, name="gated")
+            hiddens.append(first_half_of_gate(i, agg_bf))
+            if i > 0:
+                gates.append(second_half_of_gate(i - 1, hiddens[i - 1]))
+        gates.append(second_half_of_gate(len(PIECES) - 1, hiddens[-1]))
+
+        for (top, n_rows), agg, gate in zip(PIECES, aggs, gates):
+            gated = work.tile([P, n_rows * GRID_COLS], F32, name="gated")
             nc.vector.tensor_tensor(gated[:], agg[:], gate[:], ALU.mult)
-            nc.sync.dma_start(out[:, q * PIECE : (q + 1) * PIECE], gated[:])
+            nc.sync.dma_start(out[:, top * GRID_COLS : (top + n_rows) * GRID_COLS], gated[:])

@@ -11,18 +11,19 @@ TABLE_COLS = 1024
 GRID_ROWS, GRID_COLS = 32, 64
 N = GRID_ROWS * GRID_COLS
 ROW_OFFSETS = GRID_COLS // 16
+PSUM_BANKS = 8
 BANK_ROWS = 512 // GRID_COLS
 N_BANKS = GRID_ROWS // BANK_ROWS
 PIECES = ((0, 8), (8, 8), (16, 8), (24, 4), (28, 4))
+GROUPS = ((0,), (1,), (2,), (3, 4))
 
 STEP = (2, 1)
 DUO_SHIFTS = ((-4, -4), (2, 3))
 LONE_SHIFTS = ((-4, -1), (-4, 2), (-3, 4), (3, -2))
 N_SHIFTS = 2 * len(DUO_SHIFTS) + len(LONE_SHIFTS)
 REACH = 4
-LEFT = 8
 PAD_ROWS = GRID_ROWS + 2 * REACH
-PAD_COLS = LEFT + GRID_COLS + LEFT
+PAD_COLS = GRID_COLS + 2 * REACH
 N_DUO_BLOCKS = (PAD_ROWS - STEP[0] + BANK_ROWS - 1) // BANK_ROWS
 
 FLOPS = 4 * 2 * P * P * N
@@ -36,7 +37,7 @@ def shifted(padded, piece, shift):
     top, n_rows = piece
     dy, dx = shift
     row = REACH + top - dy
-    col = LEFT - dx
+    col = REACH - dx
     return padded[:, row : row + n_rows, col : col + GRID_COLS]
 
 
@@ -45,8 +46,7 @@ def tile_graphaugmentation_kernel(tc, table, wm, bm, wx, wa, bh, wz, bz, offs, o
     with (
         tc.tile_pool(name="held", bufs=1) as held,
         tc.tile_pool(name="work", bufs=len(PIECES)) as work,
-        tc.psum_pool(name="psum_hidden", bufs=len(PIECES)) as psum_hidden,
-        tc.psum_pool(name="psum_turn", bufs=8 - len(PIECES)) as psum_turn,
+        tc.psum_pool(name="psum", bufs=PSUM_BANKS) as psum,
     ):
         offsets = held.tile([P, N // 16], U16, name="offsets")
         nc.sync.dma_start(offsets[:], offs)
@@ -78,107 +78,116 @@ def tile_graphaugmentation_kernel(tc, table, wm, bm, wx, wa, bh, wz, bz, offs, o
         def picked(top, n_rows):
             return table_sb[:].indirect(offsets[:, top * ROW_OFFSETS : (top + n_rows) * ROW_OFFSETS])
 
+        msg_ps = {}
+        for b in (0, N_BANKS - 1, 1, 2):
+            msg_ps[b] = psum.tile([P, BANK_ROWS * GRID_COLS], F32, name="msg_ps", tag="bank")
+            nc.tensor.matmul(msg_ps[b][:], wm_sb[:], picked(b * BANK_ROWS, BANK_ROWS), start=True, stop=True)
+
         msg_pad = held.tile([P, PAD_ROWS, PAD_COLS], F32, name="msg_pad")
-        first, last = LEFT, LEFT + GRID_COLS
-        used = slice(first - REACH, last + REACH)
+        first, last = REACH, REACH + GRID_COLS
 
-        def make_msg_bank(b):
-            msg_ps = psum_turn.tile([P, BANK_ROWS * GRID_COLS], F32, name="msg_ps", tag="turn")
-            nc.tensor.matmul(msg_ps[:], wm_sb[:], picked(b * BANK_ROWS, BANK_ROWS), start=True, stop=True)
-            nc.scalar.activation(
-                msg_pad[:, REACH + b * BANK_ROWS : REACH + (b + 1) * BANK_ROWS, first:last],
-                as_grid(msg_ps[:]),
-                ACT.Identity,
-                bias=bm_share[:],
-                scale=share,
-            )
+        def land(b, row, n_rows, pad_row):
+            product = as_grid(msg_ps[b][:])[:, row : row + n_rows, :]
+            target = msg_pad[:, pad_row : pad_row + n_rows, :]
+            for to_cols, from_cols in (
+                (slice(first, last), slice(0, GRID_COLS)),
+                (slice(0, first), slice(GRID_COLS - REACH, GRID_COLS)),
+                (slice(last, PAD_COLS), slice(0, REACH)),
+            ):
+                nc.scalar.activation(
+                    target[:, :, to_cols], product[:, :, from_cols], ACT.Identity, bias=bm_share[:], scale=share
+                )
 
-        make_msg_bank(N_BANKS - 1)
-        make_msg_bank(0)
-        make_msg_bank(1)
+        land(0, 0, BANK_ROWS, REACH)
+        land(N_BANKS - 1, BANK_ROWS - REACH, REACH, 0)
+        land(1, 0, BANK_ROWS, REACH + BANK_ROWS)
+        land(2, 0, BANK_ROWS, REACH + 2 * BANK_ROWS)
+        land(N_BANKS - 1, 0, BANK_ROWS, REACH + (N_BANKS - 1) * BANK_ROWS)
+        land(0, 0, REACH, REACH + GRID_ROWS)
 
         hidden_ps = []
         for top, n_rows in PIECES:
-            hidden_ps.append(psum_hidden.tile([P, n_rows * GRID_COLS], F32, name="hidden_ps"))
+            hidden_ps.append(psum.tile([P, n_rows * GRID_COLS], F32, name="hidden_ps", tag="bank"))
             nc.tensor.matmul(hidden_ps[-1][:], wx_sb[:], picked(top, n_rows), start=True, stop=False)
 
-        make_msg_bank(2)
-
-
-        def pad_msg_bank(b):
-            rows = msg_pad[:, REACH + b * BANK_ROWS : REACH + (b + 1) * BANK_ROWS, :]
-            nc.vector.tensor_copy(rows[:, :, first - REACH : first], rows[:, :, last - REACH : last])
-            nc.vector.tensor_copy(rows[:, :, last : last + REACH], rows[:, :, first : first + REACH])
-            if b == N_BANKS - 1:
-                nc.vector.tensor_copy(msg_pad[:, 0:REACH, used], msg_pad[:, GRID_ROWS : GRID_ROWS + REACH, used])
-            if b == 0:
-                nc.vector.tensor_copy(
-                    msg_pad[:, REACH + GRID_ROWS : PAD_ROWS, used], msg_pad[:, REACH : 2 * REACH, used]
-                )
-
         duo_pad = held.tile([P, PAD_ROWS, PAD_COLS], F32, name="duo_pad")
-        duo_cols = slice(first - REACH + STEP[1], last + REACH)
-        back_cols = slice(first - REACH, last + REACH - STEP[1])
 
         def make_duo_block(b):
-            if b < N_BANKS - 1:
-                pad_msg_bank(b)
             top = STEP[0] + b * BANK_ROWS
             end = min(top + BANK_ROWS, PAD_ROWS)
             nc.vector.tensor_tensor(
-                duo_pad[:, top:end, duo_cols],
-                msg_pad[:, top:end, duo_cols],
-                msg_pad[:, top - STEP[0] : end - STEP[0], back_cols],
+                duo_pad[:, top:end, STEP[1] : PAD_COLS],
+                msg_pad[:, top:end, STEP[1] : PAD_COLS],
+                msg_pad[:, top - STEP[0] : end - STEP[0], 0 : PAD_COLS - STEP[1]],
                 ALU.add,
             )
 
-        def first_half_of_gate(i, agg_bf):
-            nc.tensor.matmul(hidden_ps[i][:], wa_sb[:], agg_bf[:], start=False, stop=True)
-            hidden_bf = work.tile([P, PIECES[i][1] * GRID_COLS], BF16, name="hidden_bf")
-            nc.scalar.activation(hidden_bf[:], hidden_ps[i][:], ACT.Relu, bias=bh_sb[:])
-            return hidden_bf
+        def first_half_of_gate(i):
+            nc.tensor.matmul(hidden_ps[i][:], wa_sb[:], agg_bf[i][:], start=False, stop=True)
+            hidden_bf[i] = work.tile([P, PIECES[i][1] * GRID_COLS], BF16, name="hidden_bf")
+            nc.scalar.activation(hidden_bf[i][:], hidden_ps[i][:], ACT.Relu, bias=bh_sb[:])
 
-        def second_half_of_gate(i, hidden_bf):
+        def second_half_of_gate(i):
             cells = PIECES[i][1] * GRID_COLS
-            gate_ps = psum_turn.tile([P, cells], F32, name="gate_ps", tag="turn")
-            nc.tensor.matmul(gate_ps[:], wz_sb[:], hidden_bf[:], start=True, stop=True)
-            gate = work.tile([P, cells], F32, name="gate")
-            nc.scalar.activation(gate[:], gate_ps[:], ACT.Sigmoid, bias=bz_sb[:])
-            return gate
+            gate_ps = psum.tile([P, cells], F32, name="gate_ps", tag="bank")
+            nc.tensor.matmul(gate_ps[:], wz_sb[:], hidden_bf[i][:], start=True, stop=True)
+            gate[i] = work.tile([P, cells], F32, name="gate")
+            nc.scalar.activation(gate[i][:], gate_ps[:], ACT.Sigmoid, bias=bz_sb[:])
 
-        aggs, hiddens, gates = [], [], []
-        pad_msg_bank(N_BANKS - 1)
+        lone01, lone23, duos, agg, agg_bf, hidden_bf, gate = {}, {}, {}, {}, {}, {}, {}
         make_duo_block(0)
         make_duo_block(1)
+        for g, group in enumerate(GROUPS):
+            for i in group:
+                lone01[i] = work.tile([P, PIECES[i][1] * GRID_COLS], F32, name="lone01")
+                nc.vector.tensor_tensor(
+                    as_grid(lone01[i][:]),
+                    shifted(msg_pad, PIECES[i], LONE_SHIFTS[0]),
+                    shifted(msg_pad, PIECES[i], LONE_SHIFTS[1]),
+                    ALU.add,
+                )
+            for i in group:
+                lone23[i] = work.tile([P, PIECES[i][1] * GRID_COLS], F32, name="lone23")
+                nc.vector.tensor_tensor(
+                    as_grid(lone23[i][:]),
+                    shifted(msg_pad, PIECES[i], LONE_SHIFTS[2]),
+                    shifted(msg_pad, PIECES[i], LONE_SHIFTS[3]),
+                    ALU.add,
+                )
+            for i in group:
+                duos[i] = work.tile([P, PIECES[i][1] * GRID_COLS], F32, name="duos")
+                nc.vector.tensor_tensor(
+                    as_grid(duos[i][:]),
+                    shifted(duo_pad, PIECES[i], DUO_SHIFTS[0]),
+                    shifted(duo_pad, PIECES[i], DUO_SHIFTS[1]),
+                    ALU.add,
+                )
+            for i in group:
+                nc.vector.tensor_tensor(lone01[i][:], lone01[i][:], lone23[i][:], ALU.add)
+            if g + 2 < N_DUO_BLOCKS:
+                make_duo_block(g + 2)
+            for i in group:
+                cells = PIECES[i][1] * GRID_COLS
+                agg[i] = work.tile([P, cells], F32, name="agg")
+                agg_bf[i] = work.tile([P, cells], BF16, name="agg_bf")
+                if PIECES[i][1] == BANK_ROWS:
+                    nc.vector.tensor_tensor(agg[i][:], duos[i][:], lone01[i][:], ALU.add)
+                    nc.scalar.copy(agg_bf[i][:], agg[i][:])
+                else:
+                    nc.vector.tensor_tensor(agg_bf[i][:], duos[i][:], lone01[i][:], ALU.add)
+
+            for i in group:
+                first_half_of_gate(i)
+            if g > 0:
+                for i in GROUPS[g - 1]:
+                    second_half_of_gate(i)
+        for i in GROUPS[-1]:
+            second_half_of_gate(i)
+
         for i, piece in enumerate(PIECES):
-            cells = piece[1] * GRID_COLS
-            lone01 = work.tile([P, cells], F32, name="lone01")
-            nc.vector.tensor_tensor(
-                as_grid(lone01[:]), shifted(msg_pad, piece, LONE_SHIFTS[0]), shifted(msg_pad, piece, LONE_SHIFTS[1]), ALU.add
-            )
-            lone23 = work.tile([P, cells], F32, name="lone23")
-            nc.vector.tensor_tensor(
-                as_grid(lone23[:]), shifted(msg_pad, piece, LONE_SHIFTS[2]), shifted(msg_pad, piece, LONE_SHIFTS[3]), ALU.add
-            )
-            duos = work.tile([P, cells], F32, name="duos")
-            nc.vector.tensor_tensor(
-                as_grid(duos[:]), shifted(duo_pad, piece, DUO_SHIFTS[0]), shifted(duo_pad, piece, DUO_SHIFTS[1]), ALU.add
-            )
-            nc.vector.tensor_tensor(lone01[:], lone01[:], lone23[:], ALU.add)
-            if i + 2 < N_DUO_BLOCKS:
-                make_duo_block(i + 2)
-            agg = work.tile([P, cells], F32, name="agg")
-            nc.vector.tensor_tensor(agg[:], duos[:], lone01[:], ALU.add)
-            aggs.append(agg)
-            agg_bf = work.tile([P, cells], BF16, name="agg_bf")
-            nc.vector.tensor_copy(agg_bf[:], agg[:])
-
-            hiddens.append(first_half_of_gate(i, agg_bf))
-            if i > 0:
-                gates.append(second_half_of_gate(i - 1, hiddens[i - 1]))
-        gates.append(second_half_of_gate(len(PIECES) - 1, hiddens[-1]))
-
-        for (top, n_rows), agg, gate in zip(PIECES, aggs, gates):
+            if piece[1] != BANK_ROWS:
+                nc.vector.tensor_tensor(agg[i][:], duos[i][:], lone01[i][:], ALU.add)
+        for i, (top, n_rows) in enumerate(PIECES):
             gated = work.tile([P, n_rows * GRID_COLS], F32, name="gated")
-            nc.vector.tensor_tensor(gated[:], agg[:], gate[:], ALU.mult)
+            nc.vector.tensor_tensor(gated[:], agg[i][:], gate[i][:], ALU.mult)
             nc.sync.dma_start(out[:, top * GRID_COLS : (top + n_rows) * GRID_COLS], gated[:])

@@ -79,14 +79,14 @@ def tile_graphaugmentation_kernel(tc, table, wm, bm, wx, wa, bh, wz, bz, offs, o
             return table_sb[:].indirect(offsets[:, top * ROW_OFFSETS : (top + n_rows) * ROW_OFFSETS])
 
         msg_ps = {}
-        for b in (0, N_BANKS - 1, 1, 2):
+        for b in (N_BANKS - 1, *range(N_BANKS - 1)):
             msg_ps[b] = psum.tile([P, BANK_ROWS * GRID_COLS], F32, name="msg_ps", tag="bank")
             nc.tensor.matmul(msg_ps[b][:], wm_sb[:], picked(b * BANK_ROWS, BANK_ROWS), start=True, stop=True)
 
         msg_pad = held.tile([P, PAD_ROWS, PAD_COLS], F32, name="msg_pad")
         first, last = REACH, REACH + GRID_COLS
 
-        def land(b, row, n_rows, pad_row):
+        def land(b, row, n_rows, pad_row, on_vector=False):
             product = as_grid(msg_ps[b][:])[:, row : row + n_rows, :]
             target = msg_pad[:, pad_row : pad_row + n_rows, :]
             for to_cols, from_cols in (
@@ -94,16 +94,19 @@ def tile_graphaugmentation_kernel(tc, table, wm, bm, wx, wa, bh, wz, bz, offs, o
                 (slice(0, first), slice(GRID_COLS - REACH, GRID_COLS)),
                 (slice(last, PAD_COLS), slice(0, REACH)),
             ):
-                nc.scalar.activation(
-                    target[:, :, to_cols], product[:, :, from_cols], ACT.Identity, bias=bm_share[:], scale=share
-                )
+                if on_vector:
+                    nc.vector.tensor_scalar(
+                        target[:, :, to_cols], product[:, :, from_cols], share, bm_share[:], ALU.mult, ALU.add
+                    )
+                else:
+                    nc.scalar.activation(
+                        target[:, :, to_cols], product[:, :, from_cols], ACT.Identity, bias=bm_share[:], scale=share
+                    )
 
-        land(0, 0, BANK_ROWS, REACH)
         land(N_BANKS - 1, BANK_ROWS - REACH, REACH, 0)
-        land(1, 0, BANK_ROWS, REACH + BANK_ROWS)
-        land(2, 0, BANK_ROWS, REACH + 2 * BANK_ROWS)
-        land(N_BANKS - 1, 0, BANK_ROWS, REACH + (N_BANKS - 1) * BANK_ROWS)
-        land(0, 0, REACH, REACH + GRID_ROWS)
+        land(0, 0, BANK_ROWS, REACH, on_vector=True)
+        for b in range(1, N_BANKS):
+            land(b, 0, BANK_ROWS, REACH + b * BANK_ROWS)
 
         hidden_ps = []
         for top, n_rows in PIECES:
@@ -137,6 +140,7 @@ def tile_graphaugmentation_kernel(tc, table, wm, bm, wx, wa, bh, wz, bz, offs, o
         lone01, lone23, duos, agg, agg_bf, hidden_bf, gate = {}, {}, {}, {}, {}, {}, {}
         make_duo_block(0)
         make_duo_block(1)
+        nc.vector.tensor_copy(msg_pad[:, REACH + GRID_ROWS : PAD_ROWS, :], msg_pad[:, REACH : 2 * REACH, :])
         for g, group in enumerate(GROUPS):
             for i in group:
                 lone01[i] = work.tile([P, PIECES[i][1] * GRID_COLS], F32, name="lone01")
@@ -170,7 +174,7 @@ def tile_graphaugmentation_kernel(tc, table, wm, bm, wx, wa, bh, wz, bz, offs, o
                 cells = PIECES[i][1] * GRID_COLS
                 agg[i] = work.tile([P, cells], F32, name="agg")
                 agg_bf[i] = work.tile([P, cells], BF16, name="agg_bf")
-                if PIECES[i][1] == BANK_ROWS:
+                if g < len(GROUPS) - 2:
                     nc.vector.tensor_tensor(agg[i][:], duos[i][:], lone01[i][:], ALU.add)
                     nc.scalar.copy(agg_bf[i][:], agg[i][:])
                 else:
@@ -184,8 +188,8 @@ def tile_graphaugmentation_kernel(tc, table, wm, bm, wx, wa, bh, wz, bz, offs, o
         for i in GROUPS[-1]:
             second_half_of_gate(i)
 
-        for i, piece in enumerate(PIECES):
-            if piece[1] != BANK_ROWS:
+        for group in GROUPS[-2:]:
+            for i in group:
                 nc.vector.tensor_tensor(agg[i][:], duos[i][:], lone01[i][:], ALU.add)
         for i, (top, n_rows) in enumerate(PIECES):
             gated = work.tile([P, n_rows * GRID_COLS], F32, name="gated")

@@ -26,6 +26,8 @@ PAD_ROWS = GRID_ROWS + 2 * REACH
 PAD_COLS = GRID_COLS + 2 * REACH
 N_DUO_BLOCKS = (PAD_ROWS - STEP[0] + BANK_ROWS - 1) // BANK_ROWS
 
+WARMING_MATMULS = 4
+
 FLOPS = 4 * 2 * P * P * N
 
 
@@ -67,6 +69,12 @@ def tile_graphaugmentation_kernel(tc, table, wm, bm, wx, wa, bh, wz, bz, offs, o
         wz_sb = held.tile([P, P], BF16, name="wz_sb")
         nc.sync.dma_start(wz_sb[:], wz)
 
+        zeros = held.tile([P, BANK_ROWS * GRID_COLS], BF16, name="zeros")
+        nc.gpsimd.memset(zeros[:], 0.0)
+        warming_ps = psum.tile([P, BANK_ROWS * GRID_COLS], F32, name="warming_ps", tag="bank")
+        for k in range(WARMING_MATMULS):
+            nc.tensor.matmul(warming_ps[:], zeros[:, 0:P], zeros[:], start=True, stop=True)
+
         warm = held.tile([P, 1], F32, name="warm")
         nc.vector.memset(warm[:], 0.0)
         nc.scalar.activation(warm[:], warm[:], ACT.Sigmoid)
@@ -79,14 +87,14 @@ def tile_graphaugmentation_kernel(tc, table, wm, bm, wx, wa, bh, wz, bz, offs, o
             return table_sb[:].indirect(offsets[:, top * ROW_OFFSETS : (top + n_rows) * ROW_OFFSETS])
 
         msg_ps = {}
-        for b in (N_BANKS - 1, *range(N_BANKS - 1)):
+        for b in (0, N_BANKS - 1, 1, 2):
             msg_ps[b] = psum.tile([P, BANK_ROWS * GRID_COLS], F32, name="msg_ps", tag="bank")
             nc.tensor.matmul(msg_ps[b][:], wm_sb[:], picked(b * BANK_ROWS, BANK_ROWS), start=True, stop=True)
 
         msg_pad = held.tile([P, PAD_ROWS, PAD_COLS], F32, name="msg_pad")
         first, last = REACH, REACH + GRID_COLS
 
-        def land(b, row, n_rows, pad_row, on_vector=False):
+        def land(b, row, n_rows, pad_row):
             product = as_grid(msg_ps[b][:])[:, row : row + n_rows, :]
             target = msg_pad[:, pad_row : pad_row + n_rows, :]
             for to_cols, from_cols in (
@@ -94,19 +102,16 @@ def tile_graphaugmentation_kernel(tc, table, wm, bm, wx, wa, bh, wz, bz, offs, o
                 (slice(0, first), slice(GRID_COLS - REACH, GRID_COLS)),
                 (slice(last, PAD_COLS), slice(0, REACH)),
             ):
-                if on_vector:
-                    nc.vector.tensor_scalar(
-                        target[:, :, to_cols], product[:, :, from_cols], share, bm_share[:], ALU.mult, ALU.add
-                    )
-                else:
-                    nc.scalar.activation(
-                        target[:, :, to_cols], product[:, :, from_cols], ACT.Identity, bias=bm_share[:], scale=share
-                    )
+                nc.scalar.activation(
+                    target[:, :, to_cols], product[:, :, from_cols], ACT.Identity, bias=bm_share[:], scale=share
+                )
 
+        land(0, 0, BANK_ROWS, REACH)
         land(N_BANKS - 1, BANK_ROWS - REACH, REACH, 0)
-        land(0, 0, BANK_ROWS, REACH, on_vector=True)
-        for b in range(1, N_BANKS):
-            land(b, 0, BANK_ROWS, REACH + b * BANK_ROWS)
+        land(1, 0, BANK_ROWS, REACH + BANK_ROWS)
+        land(2, 0, BANK_ROWS, REACH + 2 * BANK_ROWS)
+        land(N_BANKS - 1, 0, BANK_ROWS, REACH + (N_BANKS - 1) * BANK_ROWS)
+        land(0, 0, REACH, REACH + GRID_ROWS)
 
         hidden_ps = []
         for top, n_rows in PIECES:
@@ -140,7 +145,6 @@ def tile_graphaugmentation_kernel(tc, table, wm, bm, wx, wa, bh, wz, bz, offs, o
         lone01, lone23, duos, agg, agg_bf, hidden_bf, gate = {}, {}, {}, {}, {}, {}, {}
         make_duo_block(0)
         make_duo_block(1)
-        nc.vector.tensor_copy(msg_pad[:, REACH + GRID_ROWS : PAD_ROWS, :], msg_pad[:, REACH : 2 * REACH, :])
         for g, group in enumerate(GROUPS):
             for i in group:
                 lone01[i] = work.tile([P, PIECES[i][1] * GRID_COLS], F32, name="lone01")
@@ -174,7 +178,7 @@ def tile_graphaugmentation_kernel(tc, table, wm, bm, wx, wa, bh, wz, bz, offs, o
                 cells = PIECES[i][1] * GRID_COLS
                 agg[i] = work.tile([P, cells], F32, name="agg")
                 agg_bf[i] = work.tile([P, cells], BF16, name="agg_bf")
-                if g < len(GROUPS) - 2:
+                if PIECES[i][1] == BANK_ROWS:
                     nc.vector.tensor_tensor(agg[i][:], duos[i][:], lone01[i][:], ALU.add)
                     nc.scalar.copy(agg_bf[i][:], agg[i][:])
                 else:
@@ -188,8 +192,8 @@ def tile_graphaugmentation_kernel(tc, table, wm, bm, wx, wa, bh, wz, bz, offs, o
         for i in GROUPS[-1]:
             second_half_of_gate(i)
 
-        for group in GROUPS[-2:]:
-            for i in group:
+        for i, piece in enumerate(PIECES):
+            if piece[1] != BANK_ROWS:
                 nc.vector.tensor_tensor(agg[i][:], duos[i][:], lone01[i][:], ALU.add)
         for i, (top, n_rows) in enumerate(PIECES):
             gated = work.tile([P, n_rows * GRID_COLS], F32, name="gated")

@@ -1,4 +1,5 @@
 import concourse.mybir as mybir
+from concourse.masks import make_identity
 
 F32 = mybir.dt.float32
 BF16 = mybir.dt.bfloat16
@@ -19,14 +20,13 @@ GROUPS = ((0,), (1,), (2,), (3, 4))
 
 STEP = (2, 1)
 DUO_SHIFTS = ((-4, -4), (2, 3))
-LONE_SHIFTS = ((-4, -1), (-4, 2), (-3, 4), (3, -2))
-N_SHIFTS = 2 * len(DUO_SHIFTS) + len(LONE_SHIFTS)
+FAR_SHIFTS = ((-4, -1), (-4, 2))
+NEAR_SHIFTS = ((-3, 4), (3, -2))
+N_SHIFTS = 2 * len(DUO_SHIFTS) + len(FAR_SHIFTS) + len(NEAR_SHIFTS)
 REACH = 4
 PAD_ROWS = GRID_ROWS + 2 * REACH
 PAD_COLS = GRID_COLS + 2 * REACH
 N_DUO_BLOCKS = (PAD_ROWS - STEP[0] + BANK_ROWS - 1) // BANK_ROWS
-
-WARMING_MATMULS = 4
 
 FLOPS = 4 * 2 * P * P * N
 
@@ -69,11 +69,8 @@ def tile_graphaugmentation_kernel(tc, table, wm, bm, wx, wa, bh, wz, bz, offs, o
         wz_sb = held.tile([P, P], BF16, name="wz_sb")
         nc.sync.dma_start(wz_sb[:], wz)
 
-        zeros = held.tile([P, BANK_ROWS * GRID_COLS], BF16, name="zeros")
-        nc.gpsimd.memset(zeros[:], 0.0)
-        warming_ps = psum.tile([P, BANK_ROWS * GRID_COLS], F32, name="warming_ps", tag="bank")
-        for k in range(WARMING_MATMULS):
-            nc.tensor.matmul(warming_ps[:], zeros[:, 0:P], zeros[:], start=True, stop=True)
+        identity = held.tile([P, P], F32, name="identity")
+        make_identity(nc, identity[:])
 
         warm = held.tile([P, 1], F32, name="warm")
         nc.vector.memset(warm[:], 0.0)
@@ -130,6 +127,24 @@ def tile_graphaugmentation_kernel(tc, table, wm, bm, wx, wa, bh, wz, bz, offs, o
                 ALU.add,
             )
 
+        def sum_far_on_vector(i):
+            far[i] = work.tile([P, PIECES[i][1] * GRID_COLS], F32, name="far")
+            nc.vector.tensor_tensor(
+                as_grid(far[i][:]),
+                shifted(msg_pad, PIECES[i], FAR_SHIFTS[0]),
+                shifted(msg_pad, PIECES[i], FAR_SHIFTS[1]),
+                ALU.add,
+            )
+
+        def sum_far_on_tensor(i):
+            far[i] = psum.tile([P, PIECES[i][1] * GRID_COLS], F32, name="far_ps", tag="bank")
+            nc.tensor.matmul(
+                as_grid(far[i][:]), identity[:], shifted(msg_pad, PIECES[i], FAR_SHIFTS[0]), start=True, stop=False
+            )
+            nc.tensor.matmul(
+                as_grid(far[i][:]), identity[:], shifted(msg_pad, PIECES[i], FAR_SHIFTS[1]), start=False, stop=True
+            )
+
         def first_half_of_gate(i):
             nc.tensor.matmul(hidden_ps[i][:], wa_sb[:], agg_bf[i][:], start=False, stop=True)
             hidden_bf[i] = work.tile([P, PIECES[i][1] * GRID_COLS], BF16, name="hidden_bf")
@@ -142,24 +157,21 @@ def tile_graphaugmentation_kernel(tc, table, wm, bm, wx, wa, bh, wz, bz, offs, o
             gate[i] = work.tile([P, cells], F32, name="gate")
             nc.scalar.activation(gate[i][:], gate_ps[:], ACT.Sigmoid, bias=bz_sb[:])
 
-        lone01, lone23, duos, agg, agg_bf, hidden_bf, gate = {}, {}, {}, {}, {}, {}, {}
+        far, near, duos, agg, agg_bf, hidden_bf, gate = {}, {}, {}, {}, {}, {}, {}
         make_duo_block(0)
         make_duo_block(1)
+        for i in GROUPS[0]:
+            sum_far_on_vector(i)
         for g, group in enumerate(GROUPS):
+            if g + 1 < len(GROUPS):
+                for i in GROUPS[g + 1]:
+                    sum_far_on_tensor(i)
             for i in group:
-                lone01[i] = work.tile([P, PIECES[i][1] * GRID_COLS], F32, name="lone01")
+                near[i] = work.tile([P, PIECES[i][1] * GRID_COLS], F32, name="near")
                 nc.vector.tensor_tensor(
-                    as_grid(lone01[i][:]),
-                    shifted(msg_pad, PIECES[i], LONE_SHIFTS[0]),
-                    shifted(msg_pad, PIECES[i], LONE_SHIFTS[1]),
-                    ALU.add,
-                )
-            for i in group:
-                lone23[i] = work.tile([P, PIECES[i][1] * GRID_COLS], F32, name="lone23")
-                nc.vector.tensor_tensor(
-                    as_grid(lone23[i][:]),
-                    shifted(msg_pad, PIECES[i], LONE_SHIFTS[2]),
-                    shifted(msg_pad, PIECES[i], LONE_SHIFTS[3]),
+                    as_grid(near[i][:]),
+                    shifted(msg_pad, PIECES[i], NEAR_SHIFTS[0]),
+                    shifted(msg_pad, PIECES[i], NEAR_SHIFTS[1]),
                     ALU.add,
                 )
             for i in group:
@@ -171,7 +183,7 @@ def tile_graphaugmentation_kernel(tc, table, wm, bm, wx, wa, bh, wz, bz, offs, o
                     ALU.add,
                 )
             for i in group:
-                nc.vector.tensor_tensor(lone01[i][:], lone01[i][:], lone23[i][:], ALU.add)
+                nc.vector.tensor_tensor(near[i][:], near[i][:], far[i][:], ALU.add)
             if g + 2 < N_DUO_BLOCKS:
                 make_duo_block(g + 2)
             for i in group:
@@ -179,10 +191,10 @@ def tile_graphaugmentation_kernel(tc, table, wm, bm, wx, wa, bh, wz, bz, offs, o
                 agg[i] = work.tile([P, cells], F32, name="agg")
                 agg_bf[i] = work.tile([P, cells], BF16, name="agg_bf")
                 if PIECES[i][1] == BANK_ROWS:
-                    nc.vector.tensor_tensor(agg[i][:], duos[i][:], lone01[i][:], ALU.add)
+                    nc.vector.tensor_tensor(agg[i][:], duos[i][:], near[i][:], ALU.add)
                     nc.scalar.copy(agg_bf[i][:], agg[i][:])
                 else:
-                    nc.vector.tensor_tensor(agg_bf[i][:], duos[i][:], lone01[i][:], ALU.add)
+                    nc.vector.tensor_tensor(agg_bf[i][:], duos[i][:], near[i][:], ALU.add)
 
             for i in group:
                 first_half_of_gate(i)
@@ -194,7 +206,7 @@ def tile_graphaugmentation_kernel(tc, table, wm, bm, wx, wa, bh, wz, bz, offs, o
 
         for i, piece in enumerate(PIECES):
             if piece[1] != BANK_ROWS:
-                nc.vector.tensor_tensor(agg[i][:], duos[i][:], lone01[i][:], ALU.add)
+                nc.vector.tensor_tensor(agg[i][:], duos[i][:], near[i][:], ALU.add)
         for i, (top, n_rows) in enumerate(PIECES):
             gated = work.tile([P, n_rows * GRID_COLS], F32, name="gated")
             nc.vector.tensor_tensor(gated[:], agg[i][:], gate[i][:], ALU.mult)

@@ -15,7 +15,8 @@ ROW_OFFSETS = GRID_COLS // 16
 PSUM_BANKS = 8
 BANK_ROWS = 512 // GRID_COLS
 N_BANKS = GRID_ROWS // BANK_ROWS
-PIECES = ((0, 8), (8, 8), (16, 8), (24, 4), (28, 4))
+REACH = 4
+PIECES = ((4, 8), (12, 8), (20, 8), (28, 4), (32, 4))
 GROUPS = ((0,), (1,), (2,), (3, 4))
 
 STEP = (2, 1)
@@ -23,10 +24,8 @@ DUO_SHIFTS = ((-4, -4), (2, 3))
 FAR_SHIFTS = ((-4, -1), (-4, 2))
 NEAR_SHIFTS = ((-3, 4), (3, -2))
 N_SHIFTS = 2 * len(DUO_SHIFTS) + len(FAR_SHIFTS) + len(NEAR_SHIFTS)
-REACH = 4
 PAD_ROWS = GRID_ROWS + 2 * REACH
 PAD_COLS = GRID_COLS + 2 * REACH
-N_DUO_BLOCKS = (PAD_ROWS - STEP[0] + BANK_ROWS - 1) // BANK_ROWS
 
 FLOPS = 4 * 2 * P * P * N
 
@@ -38,7 +37,7 @@ def as_grid(flat):
 def shifted(padded, piece, shift):
     top, n_rows = piece
     dy, dx = shift
-    row = REACH + top - dy
+    row = top - dy
     col = REACH - dx
     return padded[:, row : row + n_rows, col : col + GRID_COLS]
 
@@ -84,16 +83,16 @@ def tile_graphaugmentation_kernel(tc, table, wm, bm, wx, wa, bh, wz, bz, offs, o
             return table_sb[:].indirect(offsets[:, top * ROW_OFFSETS : (top + n_rows) * ROW_OFFSETS])
 
         msg_ps = {}
-        for b in (0, N_BANKS - 1, 1, 2):
+        for b in range(N_BANKS):
             msg_ps[b] = psum.tile([P, BANK_ROWS * GRID_COLS], F32, name="msg_ps", tag="bank")
             nc.tensor.matmul(msg_ps[b][:], wm_sb[:], picked(b * BANK_ROWS, BANK_ROWS), start=True, stop=True)
 
         msg_pad = held.tile([P, PAD_ROWS, PAD_COLS], F32, name="msg_pad")
         first, last = REACH, REACH + GRID_COLS
 
-        def land(b, row, n_rows, pad_row):
-            product = as_grid(msg_ps[b][:])[:, row : row + n_rows, :]
-            target = msg_pad[:, pad_row : pad_row + n_rows, :]
+        def land(b):
+            product = as_grid(msg_ps[b][:])
+            target = msg_pad[:, b * BANK_ROWS : (b + 1) * BANK_ROWS, :]
             for to_cols, from_cols in (
                 (slice(first, last), slice(0, GRID_COLS)),
                 (slice(0, first), slice(GRID_COLS - REACH, GRID_COLS)),
@@ -103,29 +102,31 @@ def tile_graphaugmentation_kernel(tc, table, wm, bm, wx, wa, bh, wz, bz, offs, o
                     target[:, :, to_cols], product[:, :, from_cols], ACT.Identity, bias=bm_share[:], scale=share
                 )
 
-        land(0, 0, BANK_ROWS, REACH)
-        land(N_BANKS - 1, BANK_ROWS - REACH, REACH, 0)
-        land(1, 0, BANK_ROWS, REACH + BANK_ROWS)
-        land(2, 0, BANK_ROWS, REACH + 2 * BANK_ROWS)
-        land(N_BANKS - 1, 0, BANK_ROWS, REACH + (N_BANKS - 1) * BANK_ROWS)
-        land(0, 0, REACH, REACH + GRID_ROWS)
+        for b in range(N_BANKS):
+            land(b)
+        nc.scalar.copy(msg_pad[:, GRID_ROWS:PAD_ROWS, :], msg_pad[:, 0 : PAD_ROWS - GRID_ROWS, :])
 
         hidden_ps = []
         for top, n_rows in PIECES:
             hidden_ps.append(psum.tile([P, n_rows * GRID_COLS], F32, name="hidden_ps", tag="bank"))
-            nc.tensor.matmul(hidden_ps[-1][:], wx_sb[:], picked(top, n_rows), start=True, stop=False)
+            nc.tensor.matmul(hidden_ps[-1][:], wx_sb[:], picked(top % GRID_ROWS, n_rows), start=True, stop=False)
 
-        duo_pad = held.tile([P, PAD_ROWS, PAD_COLS], F32, name="duo_pad")
+        DUO_TOP = PIECES[0][0] - STEP[0]
+        duo_pad = held.tile([P, STEP[0] + GRID_ROWS, STEP[1] + GRID_COLS], F32, name="duo_pad")
 
         def make_duo_block(b):
-            top = STEP[0] + b * BANK_ROWS
-            end = min(top + BANK_ROWS, PAD_ROWS)
-            nc.vector.tensor_tensor(
-                duo_pad[:, top:end, STEP[1] : PAD_COLS],
-                msg_pad[:, top:end, STEP[1] : PAD_COLS],
-                msg_pad[:, top - STEP[0] : end - STEP[0], 0 : PAD_COLS - STEP[1]],
-                ALU.add,
-            )
+            top = PIECES[0][0] + b * BANK_ROWS - (STEP[0] if b == 0 else 0)
+            end = PIECES[0][0] + (b + 1) * BANK_ROWS
+            terms = [
+                msg_pad[:, top - dy : end - dy, REACH - STEP[1] - dx : REACH + GRID_COLS - dx]
+                for dy, dx in DUO_SHIFTS
+            ]
+            nc.vector.tensor_tensor(duo_pad[:, top - DUO_TOP : end - DUO_TOP, :], terms[0], terms[1], ALU.add)
+
+        def duo_at(piece, back):
+            row = piece[0] - DUO_TOP - STEP[0] * back
+            col = STEP[1] * (1 - back)
+            return duo_pad[:, row : row + piece[1], col : col + GRID_COLS]
 
         def sum_far_on_vector(i):
             far[i] = work.tile([P, PIECES[i][1] * GRID_COLS], F32, name="far")
@@ -159,7 +160,6 @@ def tile_graphaugmentation_kernel(tc, table, wm, bm, wx, wa, bh, wz, bz, offs, o
 
         far, near, duos, agg, agg_bf, hidden_bf, gate = {}, {}, {}, {}, {}, {}, {}
         make_duo_block(0)
-        make_duo_block(1)
         for i in GROUPS[0]:
             sum_far_on_vector(i)
         for g, group in enumerate(GROUPS):
@@ -177,15 +177,12 @@ def tile_graphaugmentation_kernel(tc, table, wm, bm, wx, wa, bh, wz, bz, offs, o
             for i in group:
                 duos[i] = work.tile([P, PIECES[i][1] * GRID_COLS], F32, name="duos")
                 nc.vector.tensor_tensor(
-                    as_grid(duos[i][:]),
-                    shifted(duo_pad, PIECES[i], DUO_SHIFTS[0]),
-                    shifted(duo_pad, PIECES[i], DUO_SHIFTS[1]),
-                    ALU.add,
+                    as_grid(duos[i][:]), duo_at(PIECES[i], 0), duo_at(PIECES[i], 1), ALU.add
                 )
             for i in group:
                 nc.vector.tensor_tensor(near[i][:], near[i][:], far[i][:], ALU.add)
-            if g + 2 < N_DUO_BLOCKS:
-                make_duo_block(g + 2)
+            if g + 1 < N_BANKS:
+                make_duo_block(g + 1)
             for i in group:
                 cells = PIECES[i][1] * GRID_COLS
                 agg[i] = work.tile([P, cells], F32, name="agg")
@@ -210,4 +207,5 @@ def tile_graphaugmentation_kernel(tc, table, wm, bm, wx, wa, bh, wz, bz, offs, o
         for i, (top, n_rows) in enumerate(PIECES):
             gated = work.tile([P, n_rows * GRID_COLS], F32, name="gated")
             nc.vector.tensor_tensor(gated[:], agg[i][:], gate[i][:], ALU.mult)
-            nc.sync.dma_start(out[:, top * GRID_COLS : (top + n_rows) * GRID_COLS], gated[:])
+            row = top % GRID_ROWS
+            nc.sync.dma_start(out[:, row * GRID_COLS : (row + n_rows) * GRID_COLS], gated[:])

@@ -17,6 +17,8 @@ BANK_ROWS = 512 // GRID_COLS
 N_BANKS = GRID_ROWS // BANK_ROWS
 REACH = 4
 PIECES = ((4, 8), (12, 8), (20, 8), (28, 4), (32, 4))
+MSG_PARTS = ((0, 8), (8, 4), (12, 4), (16, 8), (24, 8))
+FIRST_HALVES = ((4, 4), (8, 4))
 GROUPS = ((0,), (1,), (2,), (3, 4))
 
 STEP = (2, 1)
@@ -82,17 +84,18 @@ def tile_graphaugmentation_kernel(tc, table, wm, bm, wx, wa, bh, wz, bz, offs, o
         def picked(top, n_rows):
             return table_sb[:].indirect(offsets[:, top * ROW_OFFSETS : (top + n_rows) * ROW_OFFSETS])
 
-        msg_ps = {}
-        for b in range(N_BANKS):
-            msg_ps[b] = psum.tile([P, BANK_ROWS * GRID_COLS], F32, name="msg_ps", tag="bank")
-            nc.tensor.matmul(msg_ps[b][:], wm_sb[:], picked(b * BANK_ROWS, BANK_ROWS), start=True, stop=True)
+        msg_ps = []
+        for top, n_rows in MSG_PARTS:
+            msg_ps.append(psum.tile([P, n_rows * GRID_COLS], F32, name="msg_ps", tag="bank"))
+            nc.tensor.matmul(msg_ps[-1][:], wm_sb[:], picked(top, n_rows), start=True, stop=True)
 
         msg_pad = held.tile([P, PAD_ROWS, PAD_COLS], F32, name="msg_pad")
         first, last = REACH, REACH + GRID_COLS
 
-        def land(b):
-            product = as_grid(msg_ps[b][:])
-            target = msg_pad[:, b * BANK_ROWS : (b + 1) * BANK_ROWS, :]
+        def land(part):
+            top, n_rows = MSG_PARTS[part]
+            product = as_grid(msg_ps[part][:])
+            target = msg_pad[:, top : top + n_rows, :]
             for to_cols, from_cols in (
                 (slice(first, last), slice(0, GRID_COLS)),
                 (slice(0, first), slice(GRID_COLS - REACH, GRID_COLS)),
@@ -102,8 +105,8 @@ def tile_graphaugmentation_kernel(tc, table, wm, bm, wx, wa, bh, wz, bz, offs, o
                     target[:, :, to_cols], product[:, :, from_cols], ACT.Identity, bias=bm_share[:], scale=share
                 )
 
-        for b in range(N_BANKS):
-            land(b)
+        for part in range(len(MSG_PARTS)):
+            land(part)
         nc.scalar.copy(msg_pad[:, GRID_ROWS:PAD_ROWS, :], msg_pad[:, 0 : PAD_ROWS - GRID_ROWS, :])
 
         hidden_ps = []
@@ -115,8 +118,9 @@ def tile_graphaugmentation_kernel(tc, table, wm, bm, wx, wa, bh, wz, bz, offs, o
         duo_pad = held.tile([P, STEP[0] + GRID_ROWS, STEP[1] + GRID_COLS], F32, name="duo_pad")
 
         def make_duo_block(b):
-            top = PIECES[0][0] + b * BANK_ROWS - (STEP[0] if b == 0 else 0)
-            end = PIECES[0][0] + (b + 1) * BANK_ROWS
+            make_duo(PIECES[0][0] + b * BANK_ROWS, PIECES[0][0] + (b + 1) * BANK_ROWS)
+
+        def make_duo(top, end):
             terms = [
                 msg_pad[:, top - dy : end - dy, REACH - STEP[1] - dx : REACH + GRID_COLS - dx]
                 for dy, dx in DUO_SHIFTS
@@ -128,12 +132,12 @@ def tile_graphaugmentation_kernel(tc, table, wm, bm, wx, wa, bh, wz, bz, offs, o
             col = STEP[1] * (1 - back)
             return duo_pad[:, row : row + piece[1], col : col + GRID_COLS]
 
-        def sum_far_on_vector(i):
-            far[i] = work.tile([P, PIECES[i][1] * GRID_COLS], F32, name="far")
+        def pair_on_vector(pair, piece, rows, shifts):
+            at = rows[0] - piece[0]
             nc.vector.tensor_tensor(
-                as_grid(far[i][:]),
-                shifted(msg_pad, PIECES[i], FAR_SHIFTS[0]),
-                shifted(msg_pad, PIECES[i], FAR_SHIFTS[1]),
+                as_grid(pair[:])[:, at : at + rows[1], :],
+                shifted(msg_pad, rows, shifts[0]),
+                shifted(msg_pad, rows, shifts[1]),
                 ALU.add,
             )
 
@@ -159,21 +163,20 @@ def tile_graphaugmentation_kernel(tc, table, wm, bm, wx, wa, bh, wz, bz, offs, o
             nc.scalar.activation(gate[i][:], gate_ps[:], ACT.Sigmoid, bias=bz_sb[:])
 
         far, near, duos, agg, agg_bf, hidden_bf, gate = {}, {}, {}, {}, {}, {}, {}
-        make_duo_block(0)
-        for i in GROUPS[0]:
-            sum_far_on_vector(i)
+        far[0] = work.tile([P, PIECES[0][1] * GRID_COLS], F32, name="far")
+        near[0] = work.tile([P, PIECES[0][1] * GRID_COLS], F32, name="near")
+        for h, half in enumerate(FIRST_HALVES):
+            make_duo(half[0] - (STEP[0] if h == 0 else 0), half[0] + half[1])
+            pair_on_vector(far[0], PIECES[0], half, FAR_SHIFTS)
+            pair_on_vector(near[0], PIECES[0], half, NEAR_SHIFTS)
         for g, group in enumerate(GROUPS):
             if g + 1 < len(GROUPS):
                 for i in GROUPS[g + 1]:
                     sum_far_on_tensor(i)
             for i in group:
-                near[i] = work.tile([P, PIECES[i][1] * GRID_COLS], F32, name="near")
-                nc.vector.tensor_tensor(
-                    as_grid(near[i][:]),
-                    shifted(msg_pad, PIECES[i], NEAR_SHIFTS[0]),
-                    shifted(msg_pad, PIECES[i], NEAR_SHIFTS[1]),
-                    ALU.add,
-                )
+                if i > 0:
+                    near[i] = work.tile([P, PIECES[i][1] * GRID_COLS], F32, name="near")
+                    pair_on_vector(near[i], PIECES[i], PIECES[i], NEAR_SHIFTS)
             for i in group:
                 duos[i] = work.tile([P, PIECES[i][1] * GRID_COLS], F32, name="duos")
                 nc.vector.tensor_tensor(

@@ -25,6 +25,8 @@ STEP = (2, 1)
 DUO_SHIFTS = ((-4, -4), (2, 3))
 FAR_SHIFTS = ((-4, -1), (-4, 2))
 NEAR_SHIFTS = ((-3, 4), (3, -2))
+TRIO_SHIFTS = FAR_SHIFTS + NEAR_SHIFTS[:1]
+HELPED = (2, 3, 4)
 N_SHIFTS = 2 * len(DUO_SHIFTS) + len(FAR_SHIFTS) + len(NEAR_SHIFTS)
 PAD_ROWS = GRID_ROWS + 2 * REACH
 PAD_COLS = GRID_COLS + 2 * REACH
@@ -141,14 +143,16 @@ def tile_graphaugmentation_kernel(tc, table, wm, bm, wx, wa, bh, wz, bz, offs, o
                 ALU.add,
             )
 
-        def sum_far_on_tensor(i):
-            far[i] = psum.tile([P, PIECES[i][1] * GRID_COLS], F32, name="far_ps", tag="bank")
-            nc.tensor.matmul(
-                as_grid(far[i][:]), identity[:], shifted(msg_pad, PIECES[i], FAR_SHIFTS[0]), start=True, stop=False
-            )
-            nc.tensor.matmul(
-                as_grid(far[i][:]), identity[:], shifted(msg_pad, PIECES[i], FAR_SHIFTS[1]), start=False, stop=True
-            )
+        def sum_on_tensor(i, shifts):
+            helped[i] = psum.tile([P, PIECES[i][1] * GRID_COLS], F32, name="helped_ps", tag="bank")
+            for k, shift in enumerate(shifts):
+                nc.tensor.matmul(
+                    as_grid(helped[i][:]),
+                    identity[:],
+                    shifted(msg_pad, PIECES[i], shift),
+                    start=(k == 0),
+                    stop=(k == len(shifts) - 1),
+                )
 
         def first_half_of_gate(i):
             nc.tensor.matmul(hidden_ps[i][:], wa_sb[:], agg_bf[i][:], start=False, stop=True)
@@ -162,7 +166,7 @@ def tile_graphaugmentation_kernel(tc, table, wm, bm, wx, wa, bh, wz, bz, offs, o
             gate[i] = work.tile([P, cells], F32, name="gate")
             nc.scalar.activation(gate[i][:], gate_ps[:], ACT.Sigmoid, bias=bz_sb[:])
 
-        far, near, duos, agg, agg_bf, hidden_bf, gate = {}, {}, {}, {}, {}, {}, {}
+        far, near, helped, duos, agg, agg_bf, hidden_bf, gate = {}, {}, {}, {}, {}, {}, {}, {}
         far[0] = work.tile([P, PIECES[0][1] * GRID_COLS], F32, name="far")
         near[0] = work.tile([P, PIECES[0][1] * GRID_COLS], F32, name="near")
         for h, half in enumerate(FIRST_HALVES):
@@ -170,20 +174,31 @@ def tile_graphaugmentation_kernel(tc, table, wm, bm, wx, wa, bh, wz, bz, offs, o
             pair_on_vector(far[0], PIECES[0], half, FAR_SHIFTS)
             pair_on_vector(near[0], PIECES[0], half, NEAR_SHIFTS)
         for g, group in enumerate(GROUPS):
-            if g + 1 < len(GROUPS):
-                for i in GROUPS[g + 1]:
-                    sum_far_on_tensor(i)
-            for i in group:
-                if i > 0:
+            if g < len(HELPED):
+                sum_on_tensor(HELPED[g], TRIO_SHIFTS if PIECES[HELPED[g]][1] == BANK_ROWS else FAR_SHIFTS)
+            if g == 1 or g == 3:
+                for i in group:
                     near[i] = work.tile([P, PIECES[i][1] * GRID_COLS], F32, name="near")
                     pair_on_vector(near[i], PIECES[i], PIECES[i], NEAR_SHIFTS)
+            if g == 1:
+                for i in group:
+                    far[i] = work.tile([P, PIECES[i][1] * GRID_COLS], F32, name="far")
+                    pair_on_vector(far[i], PIECES[i], PIECES[i], FAR_SHIFTS)
             for i in group:
                 duos[i] = work.tile([P, PIECES[i][1] * GRID_COLS], F32, name="duos")
                 nc.vector.tensor_tensor(
                     as_grid(duos[i][:]), duo_at(PIECES[i], 0), duo_at(PIECES[i], 1), ALU.add
                 )
             for i in group:
-                nc.vector.tensor_tensor(near[i][:], near[i][:], far[i][:], ALU.add)
+                if g < 2:
+                    nc.vector.tensor_tensor(near[i][:], near[i][:], far[i][:], ALU.add)
+                elif g == 2:
+                    near[i] = work.tile([P, PIECES[i][1] * GRID_COLS], F32, name="near")
+                    nc.vector.tensor_tensor(
+                        as_grid(near[i][:]), shifted(msg_pad, PIECES[i], NEAR_SHIFTS[1]), as_grid(helped[i][:]), ALU.add
+                    )
+                else:
+                    nc.vector.tensor_tensor(near[i][:], near[i][:], helped[i][:], ALU.add)
             if g + 1 < N_BANKS:
                 make_duo_block(g + 1)
             for i in group:
@@ -196,11 +211,15 @@ def tile_graphaugmentation_kernel(tc, table, wm, bm, wx, wa, bh, wz, bz, offs, o
                 else:
                     nc.vector.tensor_tensor(agg_bf[i][:], duos[i][:], near[i][:], ALU.add)
 
-            for i in group:
-                first_half_of_gate(i)
+            if g == len(GROUPS) - 1:
+                for i in group:
+                    first_half_of_gate(i)
             if g > 0:
                 for i in GROUPS[g - 1]:
                     second_half_of_gate(i)
+            if g < len(GROUPS) - 1:
+                for i in group:
+                    first_half_of_gate(i)
         for i in GROUPS[-1]:
             second_half_of_gate(i)
 

@@ -25,8 +25,8 @@ STEP = (2, 1)
 DUO_SHIFTS = ((-4, -4), (2, 3))
 FAR_SHIFTS = ((-4, -1), (-4, 2))
 NEAR_SHIFTS = ((-3, 4), (3, -2))
-TRIO_SHIFTS = FAR_SHIFTS + NEAR_SHIFTS[:1]
-HELPED = (2, 3, 4)
+TRIO_SHIFTS = FAR_SHIFTS + NEAR_SHIFTS
+HELPED = (2,)
 N_SHIFTS = 2 * len(DUO_SHIFTS) + len(FAR_SHIFTS) + len(NEAR_SHIFTS)
 PAD_ROWS = GRID_ROWS + 2 * REACH
 PAD_COLS = GRID_COLS + 2 * REACH
@@ -180,7 +180,7 @@ def tile_graphaugmentation_kernel(tc, table, wm, bm, wx, wa, bh, wz, bz, offs, o
                 for i in group:
                     near[i] = work.tile([P, PIECES[i][1] * GRID_COLS], F32, name="near")
                     pair_on_vector(near[i], PIECES[i], PIECES[i], NEAR_SHIFTS)
-            if g == 1:
+            if g == 1 or g == 3:
                 for i in group:
                     far[i] = work.tile([P, PIECES[i][1] * GRID_COLS], F32, name="far")
                     pair_on_vector(far[i], PIECES[i], PIECES[i], FAR_SHIFTS)
@@ -190,15 +190,10 @@ def tile_graphaugmentation_kernel(tc, table, wm, bm, wx, wa, bh, wz, bz, offs, o
                     as_grid(duos[i][:]), duo_at(PIECES[i], 0), duo_at(PIECES[i], 1), ALU.add
                 )
             for i in group:
-                if g < 2:
-                    nc.vector.tensor_tensor(near[i][:], near[i][:], far[i][:], ALU.add)
-                elif g == 2:
-                    near[i] = work.tile([P, PIECES[i][1] * GRID_COLS], F32, name="near")
-                    nc.vector.tensor_tensor(
-                        as_grid(near[i][:]), shifted(msg_pad, PIECES[i], NEAR_SHIFTS[1]), as_grid(helped[i][:]), ALU.add
-                    )
+                if g == 2:
+                    near[i] = helped[i]
                 else:
-                    nc.vector.tensor_tensor(near[i][:], near[i][:], helped[i][:], ALU.add)
+                    nc.vector.tensor_tensor(near[i][:], near[i][:], far[i][:], ALU.add)
             if g + 1 < N_BANKS:
                 make_duo_block(g + 1)
             for i in group:

@@ -60,17 +60,17 @@ def tile_graphaugmentation_kernel(tc, table, wm, bm, wx, wa, bh, wz, bz, offs, o
         wm_sb = held.tile([P, P], BF16, name="wm_sb")
         nc.sync.dma_start(wm_sb[:], wm)
         bm_sb = held.tile([P, 1], F32, name="bm_sb")
-        nc.scalar.dma_start(bm_sb[:], bm)
+        nc.sync.dma_start(bm_sb[:], bm)
         wx_sb = held.tile([P, P], BF16, name="wx_sb")
         nc.sync.dma_start(wx_sb[:], wx)
-        bh_sb = held.tile([P, 1], F32, name="bh_sb")
-        nc.scalar.dma_start(bh_sb[:], bh)
         wa_sb = held.tile([P, P], BF16, name="wa_sb")
         nc.sync.dma_start(wa_sb[:], wa)
-        bz_sb = held.tile([P, 1], F32, name="bz_sb")
-        nc.scalar.dma_start(bz_sb[:], bz)
+        bh_sb = held.tile([P, 1], F32, name="bh_sb")
+        nc.sync.dma_start(bh_sb[:], bh)
         wz_sb = held.tile([P, P], BF16, name="wz_sb")
         nc.sync.dma_start(wz_sb[:], wz)
+        bz_sb = held.tile([P, 1], F32, name="bz_sb")
+        nc.sync.dma_start(bz_sb[:], bz)
 
         identity = held.tile([P, P], F32, name="identity")
         make_identity(nc, identity[:])

import concourse.mybir as mybir
from concourse.masks import make_identity

F32 = mybir.dt.float32
BF16 = mybir.dt.bfloat16
U16 = mybir.dt.uint16
ACT = mybir.ActivationFunctionType
ALU = mybir.AluOpType

P = 128
TABLE_COLS = 1024
GRID_ROWS, GRID_COLS = 32, 64
N = GRID_ROWS * GRID_COLS
ROW_OFFSETS = GRID_COLS // 16
PSUM_BANKS = 8
BANK_ROWS = 512 // GRID_COLS
N_BANKS = GRID_ROWS // BANK_ROWS
REACH = 4
PIECES = ((4, 8), (12, 8), (20, 8), (28, 4), (32, 4))
MSG_PARTS = ((0, 8), (8, 4), (12, 4), (16, 8), (24, 8))
FIRST_HALVES = ((4, 4), (8, 4))
GROUPS = ((0,), (1,), (2,), (3, 4))

STEP = (2, 1)
DUO_SHIFTS = ((-4, -4), (2, 3))
FAR_SHIFTS = ((-4, -1), (-4, 2))
NEAR_SHIFTS = ((-3, 4), (3, -2))
TRIO_SHIFTS = FAR_SHIFTS + NEAR_SHIFTS
HELPED = (2,)
N_SHIFTS = 2 * len(DUO_SHIFTS) + len(FAR_SHIFTS) + len(NEAR_SHIFTS)
PAD_ROWS = GRID_ROWS + 2 * REACH
PAD_COLS = GRID_COLS + 2 * REACH

FLOPS = 4 * 2 * P * P * N


def as_grid(flat):
    return flat.rearrange("p (r t) -> p r t", t=GRID_COLS)


def shifted(padded, piece, shift):
    top, n_rows = piece
    dy, dx = shift
    row = top - dy
    col = REACH - dx
    return padded[:, row : row + n_rows, col : col + GRID_COLS]


def tile_graphaugmentation_kernel(tc, table, wm, bm, wx, wa, bh, wz, bz, offs, out):
    nc = tc.nc
    with (
        tc.tile_pool(name="held", bufs=1) as held,
        tc.tile_pool(name="work", bufs=len(PIECES)) as work,
        tc.psum_pool(name="psum", bufs=PSUM_BANKS) as psum,
    ):
        offsets = held.tile([P, N // 16], U16, name="offsets")
        nc.sync.dma_start(offsets[:], offs)
        table_sb = held.tile([P, TABLE_COLS], BF16, name="table_sb")
        nc.scalar.dma_start(table_sb[:], table)
        wm_sb = held.tile([P, P], BF16, name="wm_sb")
        nc.sync.dma_start(wm_sb[:], wm)
        bm_sb = held.tile([P, 1], F32, name="bm_sb")
        nc.sync.dma_start(bm_sb[:], bm)
        wx_sb = held.tile([P, P], BF16, name="wx_sb")
        nc.sync.dma_start(wx_sb[:], wx)
        wa_sb = held.tile([P, P], BF16, name="wa_sb")
        nc.sync.dma_start(wa_sb[:], wa)
        bh_sb = held.tile([P, 1], F32, name="bh_sb")
        nc.sync.dma_start(bh_sb[:], bh)
        wz_sb = held.tile([P, P], BF16, name="wz_sb")
        nc.sync.dma_start(wz_sb[:], wz)
        bz_sb = held.tile([P, 1], F32, name="bz_sb")
        nc.sync.dma_start(bz_sb[:], bz)

        identity = held.tile([P, P], F32, name="identity")
        make_identity(nc, identity[:])

        warm = held.tile([P, 1], F32, name="warm")
        nc.vector.memset(warm[:], 0.0)
        nc.scalar.activation(warm[:], warm[:], ACT.Sigmoid)

        share = 1.0 / N_SHIFTS
        bm_share = held.tile([P, 1], F32, name="bm_share")
        nc.vector.tensor_scalar_mul(bm_share[:], bm_sb[:], share)

        def picked(top, n_rows):
            return table_sb[:].indirect(offsets[:, top * ROW_OFFSETS : (top + n_rows) * ROW_OFFSETS])

        msg_ps = []
        for top, n_rows in MSG_PARTS:
            msg_ps.append(psum.tile([P, n_rows * GRID_COLS], F32, name="msg_ps", tag="bank"))
            nc.tensor.matmul(msg_ps[-1][:], wm_sb[:], picked(top, n_rows), start=True, stop=True)

        msg_pad = held.tile([P, PAD_ROWS, PAD_COLS], F32, name="msg_pad")
        first, last = REACH, REACH + GRID_COLS

        def land(part):
            top, n_rows = MSG_PARTS[part]
            product = as_grid(msg_ps[part][:])
            target = msg_pad[:, top : top + n_rows, :]
            for to_cols, from_cols in (
                (slice(first, last), slice(0, GRID_COLS)),
                (slice(0, first), slice(GRID_COLS - REACH, GRID_COLS)),
                (slice(last, PAD_COLS), slice(0, REACH)),
            ):
                nc.scalar.activation(
                    target[:, :, to_cols], product[:, :, from_cols], ACT.Identity, bias=bm_share[:], scale=share
                )

        for part in range(len(MSG_PARTS)):
            land(part)
        nc.scalar.copy(msg_pad[:, GRID_ROWS:PAD_ROWS, :], msg_pad[:, 0 : PAD_ROWS - GRID_ROWS, :])

        hidden_ps = []
        for top, n_rows in PIECES:
            hidden_ps.append(psum.tile([P, n_rows * GRID_COLS], F32, name="hidden_ps", tag="bank"))
            nc.tensor.matmul(hidden_ps[-1][:], wx_sb[:], picked(top % GRID_ROWS, n_rows), start=True, stop=False)

        DUO_TOP = PIECES[0][0] - STEP[0]
        duo_pad = held.tile([P, STEP[0] + GRID_ROWS, STEP[1] + GRID_COLS], F32, name="duo_pad")

        def make_duo_block(b):
            make_duo(PIECES[0][0] + b * BANK_ROWS, PIECES[0][0] + (b + 1) * BANK_ROWS)

        def make_duo(top, end):
            terms = [
                msg_pad[:, top - dy : end - dy, REACH - STEP[1] - dx : REACH + GRID_COLS - dx]
                for dy, dx in DUO_SHIFTS
            ]
            nc.vector.tensor_tensor(duo_pad[:, top - DUO_TOP : end - DUO_TOP, :], terms[0], terms[1], ALU.add)

        def duo_at(piece, back):
            row = piece[0] - DUO_TOP - STEP[0] * back
            col = STEP[1] * (1 - back)
            return duo_pad[:, row : row + piece[1], col : col + GRID_COLS]

        def pair_on_vector(pair, piece, rows, shifts):
            at = rows[0] - piece[0]
            nc.vector.tensor_tensor(
                as_grid(pair[:])[:, at : at + rows[1], :],
                shifted(msg_pad, rows, shifts[0]),
                shifted(msg_pad, rows, shifts[1]),
                ALU.add,
            )

        def sum_on_tensor(i, shifts):
            helped[i] = psum.tile([P, PIECES[i][1] * GRID_COLS], F32, name="helped_ps", tag="bank")
            for k, shift in enumerate(shifts):
                nc.tensor.matmul(
                    as_grid(helped[i][:]),
                    identity[:],
                    shifted(msg_pad, PIECES[i], shift),
                    start=(k == 0),
                    stop=(k == len(shifts) - 1),
                )

        def first_half_of_gate(i):
            nc.tensor.matmul(hidden_ps[i][:], wa_sb[:], agg_bf[i][:], start=False, stop=True)
            hidden_bf[i] = work.tile([P, PIECES[i][1] * GRID_COLS], BF16, name="hidden_bf")
            nc.scalar.activation(hidden_bf[i][:], hidden_ps[i][:], ACT.Relu, bias=bh_sb[:])

        def second_half_of_gate(i):
            cells = PIECES[i][1] * GRID_COLS
            gate_ps = psum.tile([P, cells], F32, name="gate_ps", tag="bank")
            nc.tensor.matmul(gate_ps[:], wz_sb[:], hidden_bf[i][:], start=True, stop=True)
            gate[i] = work.tile([P, cells], F32, name="gate")
            nc.scalar.activation(gate[i][:], gate_ps[:], ACT.Sigmoid, bias=bz_sb[:])

        far, near, helped, duos, agg, agg_bf, hidden_bf, gate = {}, {}, {}, {}, {}, {}, {}, {}
        far[0] = work.tile([P, PIECES[0][1] * GRID_COLS], F32, name="far")
        near[0] = work.tile([P, PIECES[0][1] * GRID_COLS], F32, name="near")
        for h, half in enumerate(FIRST_HALVES):
            make_duo(half[0] - (STEP[0] if h == 0 else 0), half[0] + half[1])
            pair_on_vector(far[0], PIECES[0], half, FAR_SHIFTS)
            pair_on_vector(near[0], PIECES[0], half, NEAR_SHIFTS)
        for g, group in enumerate(GROUPS):
            if g < len(HELPED):
                sum_on_tensor(HELPED[g], TRIO_SHIFTS if PIECES[HELPED[g]][1] == BANK_ROWS else FAR_SHIFTS)
            if g == 1 or g == 3:
                for i in group:
                    near[i] = work.tile([P, PIECES[i][1] * GRID_COLS], F32, name="near")
                    pair_on_vector(near[i], PIECES[i], PIECES[i], NEAR_SHIFTS)
            if g == 1 or g == 3:
                for i in group:
                    far[i] = work.tile([P, PIECES[i][1] * GRID_COLS], F32, name="far")
                    pair_on_vector(far[i], PIECES[i], PIECES[i], FAR_SHIFTS)
            for i in group:
                duos[i] = work.tile([P, PIECES[i][1] * GRID_COLS], F32, name="duos")
                nc.vector.tensor_tensor(
                    as_grid(duos[i][:]), duo_at(PIECES[i], 0), duo_at(PIECES[i], 1), ALU.add
                )
            for i in group:
                if g == 2:
                    near[i] = helped[i]
                else:
                    nc.vector.tensor_tensor(near[i][:], near[i][:], far[i][:], ALU.add)
            if g + 1 < N_BANKS:
                make_duo_block(g + 1)
            for i in group:
                cells = PIECES[i][1] * GRID_COLS
                agg[i] = work.tile([P, cells], F32, name="agg")
                agg_bf[i] = work.tile([P, cells], BF16, name="agg_bf")
                if PIECES[i][1] == BANK_ROWS:
                    nc.vector.tensor_tensor(agg[i][:], duos[i][:], near[i][:], ALU.add)
                    nc.scalar.copy(agg_bf[i][:], agg[i][:])
                else:
                    nc.vector.tensor_tensor(agg_bf[i][:], duos[i][:], near[i][:], ALU.add)

            if g == len(GROUPS) - 1:
                for i in group:
                    first_half_of_gate(i)
            if g > 0:
                for i in GROUPS[g - 1]:
                    second_half_of_gate(i)
            if g < len(GROUPS) - 1:
                for i in group:
                    first_half_of_gate(i)
        for i in GROUPS[-1]:
            second_half_of_gate(i)

        for i, piece in enumerate(PIECES):
            if piece[1] != BANK_ROWS:
                nc.vector.tensor_tensor(agg[i][:], duos[i][:], near[i][:], ALU.add)
        for i, (top, n_rows) in enumerate(PIECES):
            gated = work.tile([P, n_rows * GRID_COLS], F32, name="gated")
            nc.vector.tensor_tensor(gated[:], agg[i][:], gate[i][:], ALU.mult)
            row = top % GRID_ROWS
            nc.sync.dma_start(out[:, row * GRID_COLS : (row + n_rows) * GRID_COLS], gated[:])
